import numpy as np
import ml_dtypes


def mxq(x, axis, fmt="e4m3"):
    dtype, down = {"e4m3": (ml_dtypes.float8_e4m3fn, 7), "e5m2": (ml_dtypes.float8_e5m2, 14)}[fmt]
    v = np.moveaxis(np.asarray(x, np.float32).astype(ml_dtypes.bfloat16).astype(np.float64), axis, -1)
    blocks = v.reshape(v.shape[:-1] + (-1, 32))
    amax = np.abs(blocks).max(-1, keepdims=True)
    byte = np.maximum(np.where(amax > 0, np.frexp(amax)[1] - 1 + 127, 0) - down, 1)
    scale = np.exp2(byte - 127.0)
    codes = (blocks / scale).astype(np.float32).astype(dtype).astype(np.float64)
    return np.moveaxis((codes * scale).reshape(v.shape), -1, axis)


WIDE = False


def mx_kscale(k):
    if not WIDE:
        return np.ones(k)
    levels = np.array([10, -10, 5, -5, 0])
    a = np.random.permutation(np.resize(levels, k // 512 * 4)).reshape(k // 512, 4)
    idx = np.arange(k)
    return np.exp2(a[idx // 512, idx % 128 // 32])


BF16 = ml_dtypes.bfloat16


def bf(x):
    return np.asarray(x, np.float32).astype(BF16)


def f64(x):
    return np.asarray(x).astype(np.float64)


B, L, H, D = 16, 256, 4, 128
DIM = H * D


def setup_inputs():
    r = np.random.standard_normal
    s = mx_kscale(DIM)
    ang = np.arange(L)[:, None, None] * (r((H, D)) * 0.2)[None]
    return {"x": bf(r((B, L, DIM)) * s),
            "wq_w": bf(r((DIM, DIM)) * 0.5 / np.sqrt(DIM) / s[None, :]),
            "wq_b": bf(r(DIM) * 0.1),
            "wk_w": bf(r((DIM, DIM)) * 0.5 / np.sqrt(DIM) / s[None, :]),
            "wk_b": bf(r(DIM) * 0.1),
            "rot_re": bf(np.cos(ang)),
            "rot_im": bf(np.sin(ang))}


def reference(x, wq_w, wq_b, wk_w, wk_b, rot_re, rot_im):
    xq = mxq(f64(x), 2, "e4m3")
    q = ((xq @ mxq(f64(wq_w), 1, "e4m3").T) + f64(wq_b)).reshape(B, L, H, D)
    k = ((xq @ mxq(f64(wk_w), 1, "e4m3").T) + f64(wk_b)).reshape(B, L, H, D)
    c = f64(rot_re)[None]
    sn = f64(rot_im)[None]
    return q * c, q * sn, k * c, -(k * sn)

@@ -1,0 +1,204 @@
+import concourse.mybir as mybir
+from concourse.masks import make_identity
+
+F32 = mybir.dt.float32
+BF16 = mybir.dt.bfloat16
+U32 = mybir.dt.uint32
+U8 = mybir.dt.uint8
+FP8X4 = mybir.dt.float8_e4m3fn_x4
+MULT = mybir.AluOpType.mult
+IDENTITY = mybir.ActivationFunctionType.Identity
+
+P = 128
+DIM = 512
+TOKENS = 16 * 256
+POSITIONS = 256
+SUBS = 4
+ROWS = P * SUBS
+GROUPS = TOKENS // ROWS
+WORDS = DIM // 2
+HALF = ROWS // 2
+
+FLOPS = 2 * TOKENS * DIM * (2 * DIM)
+
+
+def tile_retention_pa_t_kernel(
+    tc, x, wq_w, wq_b, wk_w, wk_b, rot_re, rot_im, out_0, out_1, out_2, out_3
+):
+    nc = tc.nc
+
+    x_rows = x.rearrange("b l k -> (b l) k")
+    outs = [
+        o.rearrange("b l h d -> (b l) (h d)").rearrange(
+            "(g p i) c -> g p (i c)", p=P, i=SUBS
+        )
+        for o in (out_0, out_1, out_2, out_3)
+    ]
+
+    with tc.manual_schedule(), tc.tile_pool(name="keep", bufs=1) as keep, tc.tile_pool(
+        name="x_in", bufs=GROUPS
+    ) as x_in, tc.tile_pool(name="stage", bufs=2) as stage, tc.tile_pool(
+        name="results", bufs=6
+    ) as results, tc.psum_pool(name="psum_words", bufs=2) as psum_words, tc.psum_pool(
+        name="psum_acc", bufs=2
+    ) as psum_acc, tc.psum_pool(name="psum_back", bufs=4) as psum_back:
+        bias_rows = keep.tile([P, P], BF16)
+        nc.vector.memset(bias_rows[:], 0.0)
+        nc.scalar.dma_start(
+            out=bias_rows[0:SUBS, :], in_=wq_b.rearrange("(m c) -> m c", c=P)
+        )
+        nc.scalar.dma_start(
+            out=bias_rows[SUBS : 2 * SUBS, :], in_=wk_b.rearrange("(m c) -> m c", c=P)
+        )
+        rot_table = keep.tile([P, 3, SUBS, DIM], BF16)
+        for plane, rot in ((0, rot_im), (1, rot_re)):
+            rot_rows = rot.rearrange("l h d -> l (h d)").rearrange(
+                "(p i) c -> p i c", i=SUBS
+            )
+            for first in (0, POSITIONS // SUBS):
+                nc.scalar.dma_start(
+                    out=rot_table[first : first + POSITIONS // SUBS, plane, :, :],
+                    in_=rot_rows,
+                )
+
+        w_raw = {}
+        x_raw = {}
+
+        def load_weight(name, w):
+            w_raw[name] = keep.tile([P, SUBS * DIM], BF16, name="w_raw_" + name)
+            nc.sync.dma_start(
+                out=w_raw[name][:].rearrange("p (m k) -> p m k", m=SUBS),
+                in_=w.rearrange("(m p) k -> p m k", p=P),
+            )
+
+        def load_tokens(g):
+            x_raw[g] = x_in.tile([P, SUBS * DIM], BF16, name="x_raw", tag="x_raw")
+            nc.sync.dma_start(
+                out=x_raw[g][:],
+                in_=x_rows[g * ROWS : (g + 1) * ROWS, :].rearrange(
+                    "(p i) k -> p (i k)", i=SUBS
+                ),
+            )
+
+        load_weight("q", wq_w)
+        load_tokens(0)
+        load_weight("k", wk_w)
+        for g in range(1, GROUPS):
+            load_tokens(g)
+
+        ident = keep.tile([P, P], F32)
+        make_identity(nc, ident[:])
+
+        def transpose_words(raw):
+            grouped = stage.tile([P, ROWS * 4], BF16, name="grouped", align_bytes=64)
+            grouped_words = grouped[:].bitcast(F32).rearrange("p (r u) -> p r u", u=2)
+            raw_words = raw[:].bitcast(F32)
+            for half in range(2):
+                words_t = psum_words.tile([P, 2, HALF], F32, name="words_t")
+                for j in range(2):
+                    sub = 2 * half + j
+                    for u in range(2):
+                        nc.tensor.transpose(
+                            words_t[:, u, j * P : (j + 1) * P],
+                            raw_words[:, sub * WORDS + u * P : sub * WORDS + (u + 1) * P],
+                            ident[:],
+                        )
+                nc.scalar.copy(
+                    out=grouped_words[:, half * HALF : (half + 1) * HALF, :],
+                    in_=words_t[:].rearrange("p u r -> p r u"),
+                )
+            return grouped
+
+        def quantise(grouped, codes, scales):
+            nc.vector.quantize_mx(
+                out=codes[:].bitcast(FP8X4), scales=scales[:], in_=grouped[:]
+            )
+
+        def project(name, bias_first, x_codes, x_scales):
+            projected = stage.tile([P, SUBS, ROWS], F32, name="projected")
+            for m in range(SUBS):
+                acc = psum_acc.tile([P, ROWS], F32, name="acc")
+                nc.tensor.matmul_mx(
+                    out=acc[:],
+                    lhsT=w_codes[name][:, m * P : (m + 1) * P].bitcast(FP8X4),
+                    lhsT_scale=w_scales[name][:, m * P : (m + 1) * P],
+                    rhs=x_codes[:].bitcast(FP8X4),
+                    rhs_scale=x_scales[:],
+                    start=True,
+                    stop=True,
+                )
+                nc.scalar.activation(
+                    out=projected[:, m, :],
+                    in_=acc[:],
+                    func=IDENTITY,
+                    bias=bias_cols[:, bias_first + m : bias_first + m + 1],
+                    scale=1.0,
+                )
+            return projected
+
+        def rotate_and_store(g, projected, first_plane, pair_outs):
+            rotated = results.tile([P, 2, SUBS, DIM], F32, name="rotated")
+            for i in range(SUBS):
+                back = psum_back.tile([P, DIM], F32, name="back")
+                for m in range(SUBS):
+                    nc.tensor.transpose(
+                        back[:, m * P : (m + 1) * P],
+                        projected[:, m, i * P : (i + 1) * P],
+                        ident[:],
+                    )
+                nc.vector.tensor_tensor(
+                    out=rotated[:, :, i, :],
+                    in0=back[:].unsqueeze(1).to_broadcast([P, 2, DIM]),
+                    in1=rot_table[:, first_plane : first_plane + 2, i, :],
+                    op=MULT,
+                )
+            for slot in range(2):
+                nc.sync.dma_start(
+                    out=pair_outs[slot][g],
+                    in_=rotated[:, slot, :, :].rearrange("p i c -> p (i c)"),
+                )
+
+        w_codes = {}
+        w_scales = {}
+        for name in ("q", "k"):
+            w_codes[name] = keep.tile([P, ROWS], U32, name="w_codes_" + name, align_bytes=64)
+            w_scales[name] = keep.tile([P, ROWS], U8, name="w_scales_" + name, align_bytes=64)
+
+        x_codes = {}
+        x_scales = {}
+
+        def quantise_tokens(g, grouped):
+            x_codes[g] = stage.tile([P, ROWS], U32, name="x_codes", align_bytes=64)
+            x_scales[g] = stage.tile([P, ROWS], U8, name="x_scales", align_bytes=64)
+            quantise(grouped, x_codes[g], x_scales[g])
+
+        grouped_wq = transpose_words(w_raw["q"])
+
+        bias_rows_f32 = keep.tile([P, P], F32)
+        nc.vector.tensor_copy(out=bias_rows_f32[:], in_=bias_rows[:])
+        bias_t = psum_words.tile([P, 2, HALF], F32, name="words_t")
+        nc.tensor.transpose(bias_t[:, 0, 0:P], bias_rows_f32[:], ident[:])
+        bias_cols = keep.tile([P, 2 * SUBS], F32)
+        nc.vector.tensor_copy(out=bias_cols[:], in_=bias_t[:, 0, 0 : 2 * SUBS])
+
+        grouped_x = {0: transpose_words(x_raw[0])}
+        quantise(grouped_wq, w_codes["q"], w_scales["q"])
+        quantise_tokens(0, grouped_x[0])
+        grouped_wk = transpose_words(w_raw["k"])
+        grouped_x[1] = transpose_words(x_raw[1])
+        quantise(grouped_wk, w_codes["k"], w_scales["k"])
+        nc.vector.tensor_scalar_mul(
+            out=rot_table[:, 2, :, :], in0=rot_table[:, 0, :, :], scalar1=-1.0
+        )
+
+        projected_q = project("q", 0, x_codes[0], x_scales[0])
+        for g in range(GROUPS):
+            if g + 1 < GROUPS:
+                quantise_tokens(g + 1, grouped_x[g + 1])
+            projected_k = project("k", SUBS, x_codes[g], x_scales[g])
+            rotate_and_store(g, projected_q, 0, (outs[1], outs[0]))
+            if g + 1 < GROUPS:
+                projected_q = project("q", 0, x_codes[g + 1], x_scales[g + 1])
+            if g + 2 < GROUPS:
+                grouped_x[g + 2] = transpose_words(x_raw[g + 2])
+            rotate_and_store(g, projected_k, 1, (outs[2], outs[3]))

@@ -18,6 +18,7 @@ ROWS = P * SUBS
 GROUPS = TOKENS // ROWS
 WORDS = DIM // 2
 HALF = ROWS // 2
+GPSIMD_SUB = 3
 
 FLOPS = 2 * TOKENS * DIM * (2 * DIM)
 
@@ -61,6 +62,10 @@ def tile_retention_pa_t_kernel(
                     in_=rot_rows,
                 )
 
+        warm = keep.tile([P, 2], F32)
+        nc.vector.memset(warm[:], 0.0)
+        nc.scalar.activation(out=warm[:, 1:2], in_=warm[:, 0:1], func=IDENTITY)
+
         w_raw = {}
         x_raw = {}
 
@@ -89,7 +94,7 @@ def tile_retention_pa_t_kernel(
         ident = keep.tile([P, P], F32)
         make_identity(nc, ident[:])
 
-        def transpose_words(raw):
+        def transpose_words(raw, copy_first_half):
             grouped = stage.tile([P, ROWS * 4], BF16, name="grouped", align_bytes=64)
             grouped_words = grouped[:].bitcast(F32).rearrange("p (r u) -> p r u", u=2)
             raw_words = raw[:].bitcast(F32)
@@ -103,7 +108,8 @@ def tile_retention_pa_t_kernel(
                             raw_words[:, sub * WORDS + u * P : sub * WORDS + (u + 1) * P],
                             ident[:],
                         )
-                nc.scalar.copy(
+                copy_out = copy_first_half if half == 0 else nc.scalar.copy
+                copy_out(
                     out=grouped_words[:, half * HALF : (half + 1) * HALF, :],
                     in_=words_t[:].rearrange("p u r -> p r u"),
                 )
@@ -136,8 +142,9 @@ def tile_retention_pa_t_kernel(
                 )
             return projected
 
-        def rotate_and_store(g, projected, first_plane, pair_outs):
+        def rotate_and_store(g, projected, first_plane, pair_outs, store_pieces):
             rotated = results.tile([P, 2, SUBS, DIM], F32, name="rotated")
+            subs_a_piece = SUBS // store_pieces
             for i in range(SUBS):
                 back = psum_back.tile([P, DIM], F32, name="back")
                 for m in range(SUBS):
@@ -146,17 +153,32 @@ def tile_retention_pa_t_kernel(
                         projected[:, m, i * P : (i + 1) * P],
                         ident[:],
                     )
-                nc.vector.tensor_tensor(
-                    out=rotated[:, :, i, :],
-                    in0=back[:].unsqueeze(1).to_broadcast([P, 2, DIM]),
-                    in1=rot_table[:, first_plane : first_plane + 2, i, :],
-                    op=MULT,
-                )
-            for slot in range(2):
-                nc.sync.dma_start(
-                    out=pair_outs[slot][g],
-                    in_=rotated[:, slot, :, :].rearrange("p i c -> p (i c)"),
-                )
+                planes = rot_table[:, first_plane : first_plane + 2, i, :]
+                if i == GPSIMD_SUB:
+                    back_sb = stage.tile([P, DIM], F32, name="back_sb")
+                    nc.scalar.copy(out=back_sb[:], in_=back[:])
+                    nc.gpsimd.tensor_tensor(
+                        out=rotated[:, :, i, :],
+                        in0=back_sb[:].unsqueeze(1).to_broadcast([P, 2, DIM]),
+                        in1=planes,
+                        op=MULT,
+                    )
+                else:
+                    nc.vector.tensor_tensor(
+                        out=rotated[:, :, i, :],
+                        in0=back[:].unsqueeze(1).to_broadcast([P, 2, DIM]),
+                        in1=planes,
+                        op=MULT,
+                    )
+                if (i + 1) % subs_a_piece == 0:
+                    piece_start = i + 1 - subs_a_piece
+                    for slot in range(2):
+                        nc.sync.dma_start(
+                            out=pair_outs[slot][g][:, piece_start * DIM : (i + 1) * DIM],
+                            in_=rotated[:, slot, piece_start : i + 1, :].rearrange(
+                                "p i c -> p (i c)"
+                            ),
+                        )
 
         w_codes = {}
         w_scales = {}
@@ -172,33 +194,35 @@ def tile_retention_pa_t_kernel(
             x_scales[g] = stage.tile([P, ROWS], U8, name="x_scales", align_bytes=64)
             quantise(grouped, x_codes[g], x_scales[g])
 
-        grouped_wq = transpose_words(w_raw["q"])
+        grouped_wq = transpose_words(w_raw["q"], nc.vector.tensor_copy)
+        grouped_x = {0: transpose_words(x_raw[0], nc.vector.tensor_copy)}
 
         bias_rows_f32 = keep.tile([P, P], F32)
         nc.vector.tensor_copy(out=bias_rows_f32[:], in_=bias_rows[:])
         bias_t = psum_words.tile([P, 2, HALF], F32, name="words_t")
         nc.tensor.transpose(bias_t[:, 0, 0:P], bias_rows_f32[:], ident[:])
+        quantise(grouped_wq, w_codes["q"], w_scales["q"])
         bias_cols = keep.tile([P, 2 * SUBS], F32)
         nc.vector.tensor_copy(out=bias_cols[:], in_=bias_t[:, 0, 0 : 2 * SUBS])
-
-        grouped_x = {0: transpose_words(x_raw[0])}
-        quantise(grouped_wq, w_codes["q"], w_scales["q"])
         quantise_tokens(0, grouped_x[0])
-        grouped_wk = transpose_words(w_raw["k"])
-        grouped_x[1] = transpose_words(x_raw[1])
+
+        grouped_wk = transpose_words(w_raw["k"], nc.vector.tensor_copy)
+        projected_q = project("q", 0, x_codes[0], x_scales[0])
         quantise(grouped_wk, w_codes["k"], w_scales["k"])
+        grouped_x[1] = transpose_words(x_raw[1], nc.vector.tensor_copy)
         nc.vector.tensor_scalar_mul(
             out=rot_table[:, 2, :, :], in0=rot_table[:, 0, :, :], scalar1=-1.0
         )
 
-        projected_q = project("q", 0, x_codes[0], x_scales[0])
         for g in range(GROUPS):
             if g + 1 < GROUPS:
                 quantise_tokens(g + 1, grouped_x[g + 1])
             projected_k = project("k", SUBS, x_codes[g], x_scales[g])
-            rotate_and_store(g, projected_q, 0, (outs[1], outs[0]))
+            rotate_and_store(
+                g, projected_q, 0, (outs[1], outs[0]), SUBS if g == 0 else 1
+            )
             if g + 1 < GROUPS:
                 projected_q = project("q", 0, x_codes[g + 1], x_scales[g + 1])
             if g + 2 < GROUPS:
-                grouped_x[g + 2] = transpose_words(x_raw[g + 2])
-            rotate_and_store(g, projected_k, 1, (outs[2], outs[3]))
+                grouped_x[g + 2] = transpose_words(x_raw[g + 2], nc.scalar.copy)
+            rotate_and_store(g, projected_k, 1, (outs[2], outs[3]), 1)

@@ -40,31 +40,17 @@ def tile_retention_pa_t_kernel(
         name="x_in", bufs=GROUPS
     ) as x_in, tc.tile_pool(name="stage", bufs=2) as stage, tc.tile_pool(
         name="results", bufs=6
-    ) as results, tc.psum_pool(name="psum_words", bufs=2) as psum_words, tc.psum_pool(
-        name="psum_acc", bufs=2
-    ) as psum_acc, tc.psum_pool(name="psum_back", bufs=4) as psum_back:
+    ) as results, tc.psum_pool(name="psum_acc", bufs=4) as psum_acc, tc.psum_pool(
+        name="psum_turned", bufs=4
+    ) as psum_turned:
         bias_rows = keep.tile([P, P], BF16)
         nc.vector.memset(bias_rows[:], 0.0)
-        nc.scalar.dma_start(
+        nc.sync.dma_start(
             out=bias_rows[0:SUBS, :], in_=wq_b.rearrange("(m c) -> m c", c=P)
         )
-        nc.scalar.dma_start(
+        nc.sync.dma_start(
             out=bias_rows[SUBS : 2 * SUBS, :], in_=wk_b.rearrange("(m c) -> m c", c=P)
         )
-        rot_table = keep.tile([P, 3, SUBS, DIM], BF16)
-        for plane, rot in ((0, rot_im), (1, rot_re)):
-            rot_rows = rot.rearrange("l h d -> l (h d)").rearrange(
-                "(p i) c -> p i c", i=SUBS
-            )
-            for first in (0, POSITIONS // SUBS):
-                nc.scalar.dma_start(
-                    out=rot_table[first : first + POSITIONS // SUBS, plane, :, :],
-                    in_=rot_rows,
-                )
-
-        warm = keep.tile([P, 2], F32)
-        nc.vector.memset(warm[:], 0.0)
-        nc.scalar.activation(out=warm[:, 1:2], in_=warm[:, 0:1], func=IDENTITY)
 
         w_raw = {}
         x_raw = {}
@@ -88,31 +74,51 @@ def tile_retention_pa_t_kernel(
         load_weight("q", wq_w)
         load_tokens(0)
         load_weight("k", wk_w)
-        for g in range(1, GROUPS):
+        load_tokens(1)
+        rot_table = keep.tile([P, 3, SUBS, DIM], BF16)
+        for plane, rot in ((0, rot_im), (1, rot_re)):
+            rot_rows = rot.rearrange("l h d -> l (h d)").rearrange(
+                "(p i) c -> p i c", i=SUBS
+            )
+            for first in (0, POSITIONS // SUBS):
+                nc.sync.dma_start(
+                    out=rot_table[first : first + POSITIONS // SUBS, plane, :, :],
+                    in_=rot_rows,
+                )
+        for g in range(2, GROUPS):
             load_tokens(g)
+
+        warm = keep.tile([P, 2], F32)
+        nc.vector.memset(warm[:], 0.0)
+        nc.scalar.activation(out=warm[:, 1:2], in_=warm[:, 0:1], func=IDENTITY)
 
         ident = keep.tile([P, P], F32)
         make_identity(nc, ident[:])
 
-        def transpose_words(raw, copy_first_half):
-            grouped = stage.tile([P, ROWS * 4], BF16, name="grouped", align_bytes=64)
+        def new_grouped():
+            return stage.tile([P, ROWS * 4], BF16, name="grouped", align_bytes=64)
+
+        def transpose_half(raw, grouped, half, copy_out):
             grouped_words = grouped[:].bitcast(F32).rearrange("p (r u) -> p r u", u=2)
             raw_words = raw[:].bitcast(F32)
-            for half in range(2):
-                words_t = psum_words.tile([P, 2, HALF], F32, name="words_t")
-                for j in range(2):
-                    sub = 2 * half + j
-                    for u in range(2):
-                        nc.tensor.transpose(
-                            words_t[:, u, j * P : (j + 1) * P],
-                            raw_words[:, sub * WORDS + u * P : sub * WORDS + (u + 1) * P],
-                            ident[:],
-                        )
-                copy_out = copy_first_half if half == 0 else nc.scalar.copy
-                copy_out(
-                    out=grouped_words[:, half * HALF : (half + 1) * HALF, :],
-                    in_=words_t[:].rearrange("p u r -> p r u"),
-                )
+            words_t = psum_turned.tile([P, 2, HALF], F32, name="turned")
+            for j in range(2):
+                sub = 2 * half + j
+                for u in range(2):
+                    nc.tensor.transpose(
+                        words_t[:, u, j * P : (j + 1) * P],
+                        raw_words[:, sub * WORDS + u * P : sub * WORDS + (u + 1) * P],
+                        ident[:],
+                    )
+            copy_out(
+                out=grouped_words[:, half * HALF : (half + 1) * HALF, :],
+                in_=words_t[:].rearrange("p u r -> p r u"),
+            )
+
+        def transpose_both_halves(raw):
+            grouped = new_grouped()
+            transpose_half(raw, grouped, 0, nc.vector.tensor_copy)
+            transpose_half(raw, grouped, 1, nc.scalar.copy)
             return grouped
 
         def quantise(grouped, codes, scales):
@@ -146,7 +152,7 @@ def tile_retention_pa_t_kernel(
             rotated = results.tile([P, 2, SUBS, DIM], F32, name="rotated")
             subs_a_piece = SUBS // store_pieces
             for i in range(SUBS):
-                back = psum_back.tile([P, DIM], F32, name="back")
+                back = psum_turned.tile([P, DIM], F32, name="turned")
                 for m in range(SUBS):
                     nc.tensor.transpose(
                         back[:, m * P : (m + 1) * P],
@@ -194,22 +200,22 @@ def tile_retention_pa_t_kernel(
             x_scales[g] = stage.tile([P, ROWS], U8, name="x_scales", align_bytes=64)
             quantise(grouped, x_codes[g], x_scales[g])
 
-        grouped_wq = transpose_words(w_raw["q"], nc.vector.tensor_copy)
-        grouped_x = {0: transpose_words(x_raw[0], nc.vector.tensor_copy)}
+        grouped_wq = transpose_both_halves(w_raw["q"])
+        grouped_x = {0: transpose_both_halves(x_raw[0])}
 
         bias_rows_f32 = keep.tile([P, P], F32)
         nc.vector.tensor_copy(out=bias_rows_f32[:], in_=bias_rows[:])
-        bias_t = psum_words.tile([P, 2, HALF], F32, name="words_t")
-        nc.tensor.transpose(bias_t[:, 0, 0:P], bias_rows_f32[:], ident[:])
+        bias_t = psum_turned.tile([P, P], F32, name="turned")
+        nc.tensor.transpose(bias_t[:], bias_rows_f32[:], ident[:])
         quantise(grouped_wq, w_codes["q"], w_scales["q"])
         bias_cols = keep.tile([P, 2 * SUBS], F32)
-        nc.vector.tensor_copy(out=bias_cols[:], in_=bias_t[:, 0, 0 : 2 * SUBS])
+        nc.vector.tensor_copy(out=bias_cols[:], in_=bias_t[:, 0 : 2 * SUBS])
         quantise_tokens(0, grouped_x[0])
 
-        grouped_wk = transpose_words(w_raw["k"], nc.vector.tensor_copy)
+        grouped_wk = transpose_both_halves(w_raw["k"])
         projected_q = project("q", 0, x_codes[0], x_scales[0])
         quantise(grouped_wk, w_codes["k"], w_scales["k"])
-        grouped_x[1] = transpose_words(x_raw[1], nc.vector.tensor_copy)
+        grouped_x[1] = transpose_both_halves(x_raw[1])
         nc.vector.tensor_scalar_mul(
             out=rot_table[:, 2, :, :], in0=rot_table[:, 0, :, :], scalar1=-1.0
         )
@@ -217,12 +223,15 @@ def tile_retention_pa_t_kernel(
         for g in range(GROUPS):
             if g + 1 < GROUPS:
                 quantise_tokens(g + 1, grouped_x[g + 1])
+            if g + 2 < GROUPS:
+                grouped_x[g + 2] = new_grouped()
+                transpose_half(x_raw[g + 2], grouped_x[g + 2], 0, nc.scalar.copy)
             projected_k = project("k", SUBS, x_codes[g], x_scales[g])
             rotate_and_store(
                 g, projected_q, 0, (outs[1], outs[0]), SUBS if g == 0 else 1
             )
+            if g + 2 < GROUPS:
+                transpose_half(x_raw[g + 2], grouped_x[g + 2], 1, nc.scalar.copy)
             if g + 1 < GROUPS:
                 projected_q = project("q", 0, x_codes[g + 1], x_scales[g + 1])
-            if g + 2 < GROUPS:
-                grouped_x[g + 2] = transpose_words(x_raw[g + 2], nc.scalar.copy)
             rotate_and_store(g, projected_k, 1, (outs[2], outs[3]), 1)

@@ -148,7 +148,7 @@ def tile_retention_pa_t_kernel(
                 )
             return projected
 
-        def rotate_and_store(g, projected, first_plane, pair_outs, store_pieces):
+        def rotate_and_store(g, projected, first_plane, pair_outs, store_pieces, gpsimd_sub):
             rotated = results.tile([P, 2, SUBS, DIM], F32, name="rotated")
             subs_a_piece = SUBS // store_pieces
             for i in range(SUBS):
@@ -160,7 +160,7 @@ def tile_retention_pa_t_kernel(
                         ident[:],
                     )
                 planes = rot_table[:, first_plane : first_plane + 2, i, :]
-                if i == GPSIMD_SUB:
+                if i == gpsimd_sub:
                     back_sb = stage.tile([P, DIM], F32, name="back_sb")
                     nc.scalar.copy(out=back_sb[:], in_=back[:])
                     nc.gpsimd.tensor_tensor(
@@ -228,10 +228,10 @@ def tile_retention_pa_t_kernel(
                 transpose_half(x_raw[g + 2], grouped_x[g + 2], 0, nc.scalar.copy)
             projected_k = project("k", SUBS, x_codes[g], x_scales[g])
             rotate_and_store(
-                g, projected_q, 0, (outs[1], outs[0]), SUBS if g == 0 else 1
+                g, projected_q, 0, (outs[1], outs[0]), SUBS if g == 0 else 1, GPSIMD_SUB
             )
             if g + 2 < GROUPS:
                 transpose_half(x_raw[g + 2], grouped_x[g + 2], 1, nc.scalar.copy)
             if g + 1 < GROUPS:
                 projected_q = project("q", 0, x_codes[g + 1], x_scales[g + 1])
-            rotate_and_store(g, projected_k, 1, (outs[2], outs[3]), 1)
+            rotate_and_store(g, projected_k, 1, (outs[2], outs[3]), 1, None)

import concourse.mybir as mybir
from concourse.masks import make_identity

F32 = mybir.dt.float32
BF16 = mybir.dt.bfloat16
U32 = mybir.dt.uint32
U8 = mybir.dt.uint8
FP8X4 = mybir.dt.float8_e4m3fn_x4
MULT = mybir.AluOpType.mult
IDENTITY = mybir.ActivationFunctionType.Identity

P = 128
DIM = 512
TOKENS = 16 * 256
POSITIONS = 256
SUBS = 4
ROWS = P * SUBS
GROUPS = TOKENS // ROWS
WORDS = DIM // 2
HALF = ROWS // 2
GPSIMD_SUB = 3

FLOPS = 2 * TOKENS * DIM * (2 * DIM)


def tile_retention_pa_t_kernel(
    tc, x, wq_w, wq_b, wk_w, wk_b, rot_re, rot_im, out_0, out_1, out_2, out_3
):
    nc = tc.nc

    x_rows = x.rearrange("b l k -> (b l) k")
    outs = [
        o.rearrange("b l h d -> (b l) (h d)").rearrange(
            "(g p i) c -> g p (i c)", p=P, i=SUBS
        )
        for o in (out_0, out_1, out_2, out_3)
    ]

    with tc.manual_schedule(), tc.tile_pool(name="keep", bufs=1) as keep, tc.tile_pool(
        name="x_in", bufs=GROUPS
    ) as x_in, tc.tile_pool(name="stage", bufs=2) as stage, tc.tile_pool(
        name="results", bufs=6
    ) as results, tc.psum_pool(name="psum_acc", bufs=4) as psum_acc, tc.psum_pool(
        name="psum_turned", bufs=4
    ) as psum_turned:
        bias_rows = keep.tile([P, P], BF16)
        nc.vector.memset(bias_rows[:], 0.0)
        nc.sync.dma_start(
            out=bias_rows[0:SUBS, :], in_=wq_b.rearrange("(m c) -> m c", c=P)
        )
        nc.sync.dma_start(
            out=bias_rows[SUBS : 2 * SUBS, :], in_=wk_b.rearrange("(m c) -> m c", c=P)
        )

        w_raw = {}
        x_raw = {}

        def load_weight(name, w):
            w_raw[name] = keep.tile([P, SUBS * DIM], BF16, name="w_raw_" + name)
            nc.sync.dma_start(
                out=w_raw[name][:].rearrange("p (m k) -> p m k", m=SUBS),
                in_=w.rearrange("(m p) k -> p m k", p=P),
            )

        def load_tokens(g):
            x_raw[g] = x_in.tile([P, SUBS * DIM], BF16, name="x_raw", tag="x_raw")
            nc.sync.dma_start(
                out=x_raw[g][:],
                in_=x_rows[g * ROWS : (g + 1) * ROWS, :].rearrange(
                    "(p i) k -> p (i k)", i=SUBS
                ),
            )

        load_weight("q", wq_w)
        load_tokens(0)
        load_weight("k", wk_w)
        load_tokens(1)
        rot_table = keep.tile([P, 3, SUBS, DIM], BF16)
        for plane, rot in ((0, rot_im), (1, rot_re)):
            rot_rows = rot.rearrange("l h d -> l (h d)").rearrange(
                "(p i) c -> p i c", i=SUBS
            )
            for first in (0, POSITIONS // SUBS):
                nc.sync.dma_start(
                    out=rot_table[first : first + POSITIONS // SUBS, plane, :, :],
                    in_=rot_rows,
                )
        for g in range(2, GROUPS):
            load_tokens(g)

        warm = keep.tile([P, 2], F32)
        nc.vector.memset(warm[:], 0.0)
        nc.scalar.activation(out=warm[:, 1:2], in_=warm[:, 0:1], func=IDENTITY)

        ident = keep.tile([P, P], F32)
        make_identity(nc, ident[:])

        def new_grouped():
            return stage.tile([P, ROWS * 4], BF16, name="grouped", align_bytes=64)

        def transpose_half(raw, grouped, half, copy_out):
            grouped_words = grouped[:].bitcast(F32).rearrange("p (r u) -> p r u", u=2)
            raw_words = raw[:].bitcast(F32)
            words_t = psum_turned.tile([P, 2, HALF], F32, name="turned")
            for j in range(2):
                sub = 2 * half + j
                for u in range(2):
                    nc.tensor.transpose(
                        words_t[:, u, j * P : (j + 1) * P],
                        raw_words[:, sub * WORDS + u * P : sub * WORDS + (u + 1) * P],
                        ident[:],
                    )
            copy_out(
                out=grouped_words[:, half * HALF : (half + 1) * HALF, :],
                in_=words_t[:].rearrange("p u r -> p r u"),
            )

        def transpose_both_halves(raw):
            grouped = new_grouped()
            transpose_half(raw, grouped, 0, nc.vector.tensor_copy)
            transpose_half(raw, grouped, 1, nc.scalar.copy)
            return grouped

        def quantise(grouped, codes, scales):
            nc.vector.quantize_mx(
                out=codes[:].bitcast(FP8X4), scales=scales[:], in_=grouped[:]
            )

        def project(name, bias_first, x_codes, x_scales):
            projected = stage.tile([P, SUBS, ROWS], F32, name="projected")
            for m in range(SUBS):
                acc = psum_acc.tile([P, ROWS], F32, name="acc")
                nc.tensor.matmul_mx(
                    out=acc[:],
                    lhsT=w_codes[name][:, m * P : (m + 1) * P].bitcast(FP8X4),
                    lhsT_scale=w_scales[name][:, m * P : (m + 1) * P],
                    rhs=x_codes[:].bitcast(FP8X4),
                    rhs_scale=x_scales[:],
                    start=True,
                    stop=True,
                )
                nc.scalar.activation(
                    out=projected[:, m, :],
                    in_=acc[:],
                    func=IDENTITY,
                    bias=bias_cols[:, bias_first + m : bias_first + m + 1],
                    scale=1.0,
                )
            return projected

        def rotate_and_store(g, projected, first_plane, pair_outs, store_pieces, gpsimd_sub):
            rotated = results.tile([P, 2, SUBS, DIM], F32, name="rotated")
            subs_a_piece = SUBS // store_pieces
            for i in range(SUBS):
                back = psum_turned.tile([P, DIM], F32, name="turned")
                for m in range(SUBS):
                    nc.tensor.transpose(
                        back[:, m * P : (m + 1) * P],
                        projected[:, m, i * P : (i + 1) * P],
                        ident[:],
                    )
                planes = rot_table[:, first_plane : first_plane + 2, i, :]
                if i == gpsimd_sub:
                    back_sb = stage.tile([P, DIM], F32, name="back_sb")
                    nc.scalar.copy(out=back_sb[:], in_=back[:])
                    nc.gpsimd.tensor_tensor(
                        out=rotated[:, :, i, :],
                        in0=back_sb[:].unsqueeze(1).to_broadcast([P, 2, DIM]),
                        in1=planes,
                        op=MULT,
                    )
                else:
                    nc.vector.tensor_tensor(
                        out=rotated[:, :, i, :],
                        in0=back[:].unsqueeze(1).to_broadcast([P, 2, DIM]),
                        in1=planes,
                        op=MULT,
                    )
                if (i + 1) % subs_a_piece == 0:
                    piece_start = i + 1 - subs_a_piece
                    for slot in range(2):
                        nc.sync.dma_start(
                            out=pair_outs[slot][g][:, piece_start * DIM : (i + 1) * DIM],
                            in_=rotated[:, slot, piece_start : i + 1, :].rearrange(
                                "p i c -> p (i c)"
                            ),
                        )

        w_codes = {}
        w_scales = {}
        for name in ("q", "k"):
            w_codes[name] = keep.tile([P, ROWS], U32, name="w_codes_" + name, align_bytes=64)
            w_scales[name] = keep.tile([P, ROWS], U8, name="w_scales_" + name, align_bytes=64)

        x_codes = {}
        x_scales = {}

        def quantise_tokens(g, grouped):
            x_codes[g] = stage.tile([P, ROWS], U32, name="x_codes", align_bytes=64)
            x_scales[g] = stage.tile([P, ROWS], U8, name="x_scales", align_bytes=64)
            quantise(grouped, x_codes[g], x_scales[g])

        grouped_wq = transpose_both_halves(w_raw["q"])
        grouped_x = {0: transpose_both_halves(x_raw[0])}

        bias_rows_f32 = keep.tile([P, P], F32)
        nc.vector.tensor_copy(out=bias_rows_f32[:], in_=bias_rows[:])
        bias_t = psum_turned.tile([P, P], F32, name="turned")
        nc.tensor.transpose(bias_t[:], bias_rows_f32[:], ident[:])
        quantise(grouped_wq, w_codes["q"], w_scales["q"])
        bias_cols = keep.tile([P, 2 * SUBS], F32)
        nc.vector.tensor_copy(out=bias_cols[:], in_=bias_t[:, 0 : 2 * SUBS])
        quantise_tokens(0, grouped_x[0])

        grouped_wk = transpose_both_halves(w_raw["k"])
        projected_q = project("q", 0, x_codes[0], x_scales[0])
        quantise(grouped_wk, w_codes["k"], w_scales["k"])
        grouped_x[1] = transpose_both_halves(x_raw[1])
        nc.vector.tensor_scalar_mul(
            out=rot_table[:, 2, :, :], in0=rot_table[:, 0, :, :], scalar1=-1.0
        )

        for g in range(GROUPS):
            if g + 1 < GROUPS:
                quantise_tokens(g + 1, grouped_x[g + 1])
            if g + 2 < GROUPS:
                grouped_x[g + 2] = new_grouped()
                transpose_half(x_raw[g + 2], grouped_x[g + 2], 0, nc.scalar.copy)
            projected_k = project("k", SUBS, x_codes[g], x_scales[g])
            rotate_and_store(
                g, projected_q, 0, (outs[1], outs[0]), SUBS if g == 0 else 1, GPSIMD_SUB
            )
            if g + 2 < GROUPS:
                transpose_half(x_raw[g + 2], grouped_x[g + 2], 1, nc.scalar.copy)
            if g + 1 < GROUPS:
                projected_q = project("q", 0, x_codes[g + 1], x_scales[g + 1])
            rotate_and_store(g, projected_k, 1, (outs[2], outs[3]), 1, None)
